import numpy as np
import ml_dtypes


def mxq(x, axis, fmt="e4m3"):
    dtype, down = {"e4m3": (ml_dtypes.float8_e4m3fn, 7), "e5m2": (ml_dtypes.float8_e5m2, 14)}[fmt]
    v = np.moveaxis(np.asarray(x, np.float32).astype(ml_dtypes.bfloat16).astype(np.float64), axis, -1)
    blocks = v.reshape(v.shape[:-1] + (-1, 32))
    amax = np.abs(blocks).max(-1, keepdims=True)
    byte = np.maximum(np.where(amax > 0, np.frexp(amax)[1] - 1 + 127, 0) - down, 1)
    scale = np.exp2(byte - 127.0)
    codes = (blocks / scale).astype(np.float32).astype(dtype).astype(np.float64)
    return np.moveaxis((codes * scale).reshape(v.shape), -1, axis)


WIDE = False


def mx_kscale(k):
    if not WIDE:
        return np.ones(k)
    levels = np.array([10, -10, 5, -5, 0])
    a = np.random.permutation(np.resize(levels, k // 512 * 4)).reshape(k // 512, 4)
    idx = np.arange(k)
    return np.exp2(a[idx // 512, idx % 128 // 32])


BF16 = ml_dtypes.bfloat16


def bf(x):
    return np.asarray(x, np.float32).astype(BF16)


def f64(x):
    return np.asarray(x).astype(np.float64)


E2M1 = np.array([0.0, 0.5, 1.0, 1.5, 2.0, 3.0, 4.0, 6.0, -0.0, -0.5, -1.0, -1.5, -2.0, -3.0, -4.0, -6.0])


def pack_weight(w, fmt):
    k, n = w.shape
    w = f64(bf(w)).reshape(k // 32, 32, n)
    amax = np.abs(w).max(1)
    if fmt == "e4m3":
        byte = np.frexp(amax)[1] - 1 + 127 - 7
    else:
        mant, ex = np.frexp(amax / 6.0)
        byte = np.where(mant > 0.5, ex, ex - 1) + 127
    byte = np.clip(np.where(amax > 0, byte, 1), 1, 254)
    scaled = (w * np.exp2(127.0 - byte)[:, None, :]).reshape(k, n).astype(np.float32)
    by_word = np.ascontiguousarray(scaled.reshape(k // 512, 128, 4, n).transpose(0, 1, 3, 2))
    if fmt == "e4m3":
        words = by_word.astype(ml_dtypes.float8_e4m3fn).view(np.uint8)
    else:
        c = by_word.astype(ml_dtypes.float4_e2m1fn).view(np.uint8) & 0xF
        words = c[..., 0::2] | (c[..., 1::2] << 4)
    return np.ascontiguousarray(words), np.ascontiguousarray(byte.astype(np.uint8).reshape(k // 512, 16, n))


def unpack_weight(words, scales, fmt):
    g, p, n, _ = words.shape
    if fmt == "e4m3":
        vals = np.ascontiguousarray(words).view(ml_dtypes.float8_e4m3fn).astype(np.float64)
    else:
        nib = np.empty((g, p, n, 4), np.uint8)
        nib[..., 0::2] = words & 0xF
        nib[..., 1::2] = words >> 4
        vals = E2M1[nib]
    vals = vals * np.repeat(np.exp2(scales.astype(np.float64) - 127.0), 8, axis=1)[..., None]
    return vals.transpose(0, 1, 3, 2).reshape(g * 512, n)

def pack4(w):
    words, scales = pack_weight(w, "e2m1")
    return words.reshape(words.shape[0], 128, -1), scales


def unpack4(words, scales):
    return unpack_weight(words.reshape(words.shape[0], 128, -1, 2), scales, "e2m1")


B, S, D, NH, NKV, HD, QB = 1, 128, 512, 16, 4, 128, 512
Q_DIM = NH * HD
KV_DIM = NKV * HD


def rot(t, f0, f1):
    tp = t.reshape(t.shape[:-1] + (HD // 2, 2))
    t0, t1 = tp[..., 0], tp[..., 1]
    row1 = t0 * f0 + t1 * f1
    row0 = t0 * f1 - t1 * f0
    return np.stack([row0, row1], axis=-1).reshape(t.shape)


def setup_inputs():
    s = mx_kscale(D)
    x = bf(np.random.standard_normal((B, S, D)) * s)
    freqs_cis = bf(np.random.standard_normal((S, HD)))
    w = np.random.standard_normal((Q_DIM + 2 * KV_DIM, D)) / np.sqrt(D) / s
    words, scales = pack4(np.ascontiguousarray(w.T))
    return {"x": x,
            "freqs_cis": freqs_cis,
            "Wqkv_words": words,
            "Wqkv_scales": scales}


def reference(x, freqs_cis, Wqkv_words, Wqkv_scales):
    xqkv = mxq(f64(x), 2, "e4m3") @ unpack4(Wqkv_words, Wqkv_scales)
    xq = xqkv[..., :Q_DIM].reshape(B, S, NH, HD)
    xk = xqkv[..., Q_DIM:Q_DIM + KV_DIM].reshape(B, S, NKV, HD)
    xv = xqkv[..., Q_DIM + KV_DIM:].reshape(B, S, NKV, HD)
    f = f64(freqs_cis).reshape(S, 1, HD // 2, 2)
    f0, f1 = f[..., 0], f[..., 1]
    q_rot = rot(xq, f0, f1).transpose(0, 2, 1, 3)
    k_rot = rot(xk, f0, f1).transpose(0, 2, 1, 3)
    v = xv.transpose(0, 2, 1, 3)
    return q_rot, k_rot, v

@@ -1,0 +1,133 @@
+from contextlib import ExitStack
+
+import concourse.mybir as mybir
+from concourse.masks import make_identity
+
+F32 = mybir.dt.float32
+BF16 = mybir.dt.bfloat16
+I32 = mybir.dt.int32
+U32 = mybir.dt.uint32
+U8 = mybir.dt.uint8
+FP8X4 = mybir.dt.float8_e4m3fn_x4
+FP4X4 = mybir.dt.float4_e2m1fn_x4
+
+P = 128
+D = 512
+HD = 128
+PAIRS = HD // 2
+BANK = 512
+HEADS_PER_BANK = BANK // HD
+Q_BANKS = 4
+ROTARY_BANKS = Q_BANKS + 1
+BANKS = ROTARY_BANKS + 1
+N_ALL = BANKS * BANK
+WORD_BYTES = 2
+
+FLOPS = 2 * P * D * N_ALL
+
+
+def tile_rlaattention_pa_s_kernel(
+    tc, x, freqs_cis, Wqkv_words, Wqkv_scales, out_0, out_1, out_2
+):
+    nc = tc.nc
+    with ExitStack() as ctx:
+        keep = ctx.enter_context(tc.tile_pool(name="keep", bufs=1))
+        psum = ctx.enter_context(tc.psum_pool(name="psum", bufs=1))
+
+        w_scales = keep.tile([P, N_ALL], U8, align_bytes=64)
+        nc.vector.memset(w_scales[:].bitcast(I32), 0)
+
+        x_sb = keep.tile([P, D], BF16)
+        nc.sync.dma_start(out=x_sb[:], in_=x[0])
+        f_sb = keep.tile([P, HD], BF16)
+        nc.scalar.dma_start(out=f_sb[:], in_=freqs_cis)
+
+        w_words = keep.tile([P, WORD_BYTES * N_ALL], U8, align_bytes=64)
+
+        def load_words(first_bank, end_bank):
+            cols = slice(WORD_BYTES * BANK * first_bank, WORD_BYTES * BANK * end_bank)
+            nc.sync.dma_start(
+                out=w_words[:, cols].bitcast(I32), in_=Wqkv_words[0][:, cols].bitcast(I32)
+            )
+
+        load_words(0, 1)
+        for quadrant in range(4):
+            nc.sync.dma_start(
+                out=w_scales[32 * quadrant : 32 * quadrant + 4, :].bitcast(I32),
+                in_=Wqkv_scales[0, 4 * quadrant : 4 * quadrant + 4, :].bitcast(I32),
+            )
+        load_words(1, 3)
+        load_words(3, BANKS)
+
+        ident = keep.tile([P, P], F32)
+        make_identity(nc, ident[:])
+        x_words = x_sb[:].bitcast(F32)
+        xt = psum.tile([P, 2, P], F32)
+        for u in range(2):
+            nc.tensor.transpose(xt[:, u, :], x_words[:, u : D // 2 : 2], ident[:])
+        x_grouped = keep.tile([P, P, 2], F32, align_bytes=64)
+        nc.vector.tensor_copy(out=x_grouped[:], in_=xt[:].rearrange("p u s -> p s u"))
+        x_codes = keep.tile([P, P], U32, align_bytes=64)
+        x_scales = keep.tile([P, P], U8, align_bytes=64)
+        nc.vector.quantize_mx(
+            out=x_codes[:].bitcast(FP8X4),
+            scales=x_scales[:],
+            in_=x_grouped[:].rearrange("p s u -> p (s u)").bitcast(BF16),
+        )
+
+        f_pairs = f_sb[:].rearrange("s (j e) -> s j e", e=2)
+        same = keep.tile([P, PAIRS, 2], F32)
+        nc.scalar.copy(out=same[:], in_=f_pairs[:, :, 1:2].to_broadcast([P, PAIRS, 2]))
+        cross = keep.tile([P, PAIRS, 2], F32)
+        nc.scalar.mul(out=cross[:, :, 0:1], in_=f_pairs[:, :, 0:1], mul=-1.0)
+        nc.scalar.copy(out=cross[:, :, 1:2], in_=f_pairs[:, :, 0:1])
+        by_head = [P, HEADS_PER_BANK, PAIRS, 2]
+        same_by_head = same[:].unsqueeze(1).to_broadcast(by_head)
+        cross_by_head = cross[:].unsqueeze(1).to_broadcast(by_head)
+
+        banks = []
+        for b in range(BANKS):
+            acc = psum.tile([P, BANK], F32, name="acc%d" % b)
+            nc.tensor.matmul_mx(
+                out=acc[:],
+                lhsT=x_codes[:].bitcast(FP8X4),
+                lhsT_scale=x_scales[:],
+                rhs=w_words[:, WORD_BYTES * BANK * b : WORD_BYTES * BANK * (b + 1)].bitcast(FP4X4),
+                rhs_scale=w_scales[:, BANK * b : BANK * (b + 1)],
+                start=True,
+                stop=True,
+            )
+            banks.append(acc)
+
+        homes = [out_0[0, HEADS_PER_BANK * b : HEADS_PER_BANK * (b + 1)] for b in range(Q_BANKS)]
+        homes.append(out_1[0])
+        homes.append(out_2[0])
+
+        def store(b, result):
+            nc.sync.dma_start(
+                out=homes[b].rearrange("h s f -> s h f"),
+                in_=result[:].rearrange("s (h f) -> s h f", h=HEADS_PER_BANK),
+            )
+
+        values = keep.tile([P, BANK], F32)
+        nc.scalar.copy(out=values[:], in_=banks[ROTARY_BANKS][:])
+        store(ROTARY_BANKS, values)
+
+        for b in range(ROTARY_BANKS):
+            t = banks[b][:].rearrange("s (h j e) -> s h j e", h=HEADS_PER_BANK, e=2)
+            straight = keep.tile([P, BANK], F32, name="straight%d" % b)
+            crossed = keep.tile([P, BANK], F32, name="crossed%d" % b)
+            as_pairs = "s (h j e) -> s h j e"
+            nc.vector.tensor_mul(
+                out=straight[:].rearrange(as_pairs, h=HEADS_PER_BANK, e=2),
+                in0=t,
+                in1=same_by_head,
+            )
+            nc.vector.tensor_mul(
+                out=crossed[:].rearrange(as_pairs, h=HEADS_PER_BANK, e=2),
+                in0=t[:, :, :, ::-1],
+                in1=cross_by_head,
+            )
+            adder = nc.gpsimd if b < ROTARY_BANKS - 1 else nc.vector
+            adder.tensor_add(out=straight[:], in0=straight[:], in1=crossed[:])
+            store(b, straight)

@@ -22,6 +22,7 @@ ROTARY_BANKS = Q_BANKS + 1
 BANKS = ROTARY_BANKS + 1
 N_ALL = BANKS * BANK
 WORD_BYTES = 2
+PE_SUM_BANK = 1
 
 FLOPS = 2 * P * D * N_ALL
 
@@ -128,6 +129,23 @@ def tile_rlaattention_pa_s_kernel(
                 in0=t[:, :, :, ::-1],
                 in1=cross_by_head,
             )
-            adder = nc.gpsimd if b < ROTARY_BANKS - 1 else nc.vector
-            adder.tensor_add(out=straight[:], in0=straight[:], in1=crossed[:])
-            store(b, straight)
+            if b == PE_SUM_BANK:
+                total = psum.tile([P, BANK], F32, name="total")
+                nc.tensor.matmul(out=total[:], lhsT=ident[:], rhs=straight[:], start=True, stop=False)
+                nc.tensor.matmul(out=total[:], lhsT=ident[:], rhs=crossed[:], start=False, stop=True)
+                summed = keep.tile([P, BANK], F32, name="summed")
+                nc.scalar.copy(out=summed[:], in_=total[:])
+                store(b, summed)
+                continue
+            if b < ROTARY_BANKS - 1:
+                nc.gpsimd.tensor_add(out=straight[:], in0=straight[:], in1=crossed[:])
+                store(b, straight)
+            else:
+                half_heads = HEADS_PER_BANK // 2
+                for part in range(2):
+                    cols = slice(part * BANK // 2, (part + 1) * BANK // 2)
+                    nc.vector.tensor_add(out=straight[:, cols], in0=straight[:, cols], in1=crossed[:, cols])
+                    nc.sync.dma_start(
+                        out=homes[b][part * half_heads : (part + 1) * half_heads].rearrange("h s f -> s h f"),
+                        in_=straight[:, cols].rearrange("s (h f) -> s h f", h=half_heads),
+                    )

@@ -38,6 +38,10 @@ def tile_rlaattention_pa_s_kernel(
         w_scales = keep.tile([P, N_ALL], U8, align_bytes=64)
         nc.vector.memset(w_scales[:].bitcast(I32), 0)
 
+        signs = keep.tile([P, PAIRS, 2], F32)
+        nc.vector.memset(signs[:, :, 0:1], -1.0)
+        nc.vector.memset(signs[:, :, 1:2], 1.0)
+
         x_sb = keep.tile([P, D], BF16)
         nc.sync.dma_start(out=x_sb[:], in_=x[0])
         f_sb = keep.tile([P, HD], BF16)
@@ -63,11 +67,11 @@ def tile_rlaattention_pa_s_kernel(
         ident = keep.tile([P, P], F32)
         make_identity(nc, ident[:])
         x_words = x_sb[:].bitcast(F32)
-        xt = psum.tile([P, 2, P], F32)
+        xt = psum.tile([P, 2, P], F32, tag="spare")
         for u in range(2):
             nc.tensor.transpose(xt[:, u, :], x_words[:, u : D // 2 : 2], ident[:])
         x_grouped = keep.tile([P, P, 2], F32, align_bytes=64)
-        nc.vector.tensor_copy(out=x_grouped[:], in_=xt[:].rearrange("p u s -> p s u"))
+        nc.scalar.copy(out=x_grouped[:], in_=xt[:].rearrange("p u s -> p s u"))
         x_codes = keep.tile([P, P], U32, align_bytes=64)
         x_scales = keep.tile([P, P], U8, align_bytes=64)
         nc.vector.quantize_mx(
@@ -78,27 +82,31 @@ def tile_rlaattention_pa_s_kernel(
 
         f_pairs = f_sb[:].rearrange("s (j e) -> s j e", e=2)
         same = keep.tile([P, PAIRS, 2], F32)
-        nc.scalar.copy(out=same[:], in_=f_pairs[:, :, 1:2].to_broadcast([P, PAIRS, 2]))
+        nc.vector.tensor_copy(out=same[:], in_=f_pairs[:, :, 1:2].to_broadcast([P, PAIRS, 2]))
         cross = keep.tile([P, PAIRS, 2], F32)
-        nc.scalar.mul(out=cross[:, :, 0:1], in_=f_pairs[:, :, 0:1], mul=-1.0)
-        nc.scalar.copy(out=cross[:, :, 1:2], in_=f_pairs[:, :, 0:1])
-        by_head = [P, HEADS_PER_BANK, PAIRS, 2]
-        same_by_head = same[:].unsqueeze(1).to_broadcast(by_head)
-        cross_by_head = cross[:].unsqueeze(1).to_broadcast(by_head)
+        nc.vector.tensor_mul(out=cross[:], in0=f_pairs[:, :, 0:1].to_broadcast([P, PAIRS, 2]), in1=signs[:])
 
         banks = []
         for b in range(BANKS):
-            acc = psum.tile([P, BANK], F32, name="acc%d" % b)
-            nc.tensor.matmul_mx(
-                out=acc[:],
-                lhsT=x_codes[:].bitcast(FP8X4),
-                lhsT_scale=x_scales[:],
-                rhs=w_words[:, WORD_BYTES * BANK * b : WORD_BYTES * BANK * (b + 1)].bitcast(FP4X4),
-                rhs_scale=w_scales[:, BANK * b : BANK * (b + 1)],
-                start=True,
-                stop=True,
-            )
-            banks.append(acc)
+            widths = [HD, HD, BANK // 2] if b == 0 else [BANK]
+            pieces = []
+            for width in widths:
+                first = sum(piece[1] for piece in pieces)
+                cols = slice(BANK * b + first, BANK * b + first + width)
+                acc = psum.tile(
+                    [P, width], F32, name="acc%d_%d" % (b, first), tag="spare" if cols.start == 0 else "acc%d_%d" % (b, first)
+                )
+                nc.tensor.matmul_mx(
+                    out=acc[:],
+                    lhsT=x_codes[:].bitcast(FP8X4),
+                    lhsT_scale=x_scales[:],
+                    rhs=w_words[:, WORD_BYTES * cols.start : WORD_BYTES * cols.stop].bitcast(FP4X4),
+                    rhs_scale=w_scales[:, cols],
+                    start=True,
+                    stop=True,
+                )
+                pieces.append((first, width, acc))
+            banks.append(pieces)
 
         homes = [out_0[0, HEADS_PER_BANK * b : HEADS_PER_BANK * (b + 1)] for b in range(Q_BANKS)]
         homes.append(out_1[0])
@@ -111,26 +119,28 @@ def tile_rlaattention_pa_s_kernel(
             )
 
         values = keep.tile([P, BANK], F32)
-        nc.scalar.copy(out=values[:], in_=banks[ROTARY_BANKS][:])
+        nc.scalar.copy(out=values[:], in_=banks[ROTARY_BANKS][0][2][:])
         store(ROTARY_BANKS, values)
 
         for b in range(ROTARY_BANKS):
-            t = banks[b][:].rearrange("s (h j e) -> s h j e", h=HEADS_PER_BANK, e=2)
             straight = keep.tile([P, BANK], F32, name="straight%d" % b)
             crossed = keep.tile([P, BANK], F32, name="crossed%d" % b)
             as_pairs = "s (h j e) -> s h j e"
-            nc.vector.tensor_mul(
-                out=straight[:].rearrange(as_pairs, h=HEADS_PER_BANK, e=2),
-                in0=t,
-                in1=same_by_head,
-            )
-            nc.vector.tensor_mul(
-                out=crossed[:].rearrange(as_pairs, h=HEADS_PER_BANK, e=2),
-                in0=t[:, :, :, ::-1],
-                in1=cross_by_head,
-            )
+            for first, width, acc in banks[b]:
+                heads = width // HD
+                t = acc[:].rearrange(as_pairs, h=heads, e=2)
+                nc.vector.tensor_mul(
+                    out=straight[:, first : first + width].rearrange(as_pairs, h=heads, e=2),
+                    in0=t,
+                    in1=same[:].unsqueeze(1).to_broadcast([P, heads, PAIRS, 2]),
+                )
+                nc.vector.tensor_mul(
+                    out=crossed[:, first : first + width].rearrange(as_pairs, h=heads, e=2),
+                    in0=t[:, :, :, ::-1],
+                    in1=cross[:].unsqueeze(1).to_broadcast([P, heads, PAIRS, 2]),
+                )
             if b == PE_SUM_BANK:
-                total = psum.tile([P, BANK], F32, name="total")
+                total = psum.tile([P, BANK], F32, name="total", tag="spare")
                 nc.tensor.matmul(out=total[:], lhsT=ident[:], rhs=straight[:], start=True, stop=False)
                 nc.tensor.matmul(out=total[:], lhsT=ident[:], rhs=crossed[:], start=False, stop=True)
                 summed = keep.tile([P, BANK], F32, name="summed")

@@ -112,50 +112,53 @@ def tile_rlaattention_pa_s_kernel(
         homes.append(out_1[0])
         homes.append(out_2[0])
 
-        def store(b, result):
+        def store(b, first, result):
+            heads = result.shape[1] // HD
             nc.sync.dma_start(
-                out=homes[b].rearrange("h s f -> s h f"),
-                in_=result[:].rearrange("s (h f) -> s h f", h=HEADS_PER_BANK),
+                out=homes[b][first // HD : first // HD + heads].rearrange("h s f -> s h f"),
+                in_=result[:].rearrange("s (h f) -> s h f", h=heads),
             )
 
         values = keep.tile([P, BANK], F32)
         nc.scalar.copy(out=values[:], in_=banks[ROTARY_BANKS][0][2][:])
-        store(ROTARY_BANKS, values)
+        store(ROTARY_BANKS, 0, values)
 
-        for b in range(ROTARY_BANKS):
-            straight = keep.tile([P, BANK], F32, name="straight%d" % b)
-            crossed = keep.tile([P, BANK], F32, name="crossed%d" % b)
-            as_pairs = "s (h j e) -> s h j e"
-            for first, width, acc in banks[b]:
-                heads = width // HD
-                t = acc[:].rearrange(as_pairs, h=heads, e=2)
+        as_pairs = "s (h j e) -> s h j e"
+
+        def products(b, first, width):
+            straight = keep.tile([P, width], F32, name="straight%d_%d" % (b, first))
+            crossed = keep.tile([P, width], F32, name="crossed%d_%d" % (b, first))
+            for piece_first, piece_width, acc in banks[b]:
+                lo = max(first, piece_first)
+                hi = min(first + width, piece_first + piece_width)
+                if lo >= hi:
+                    continue
+                heads = (hi - lo) // HD
+                t = acc[:, lo - piece_first : hi - piece_first].rearrange(as_pairs, h=heads, e=2)
                 nc.vector.tensor_mul(
-                    out=straight[:, first : first + width].rearrange(as_pairs, h=heads, e=2),
+                    out=straight[:, lo - first : hi - first].rearrange(as_pairs, h=heads, e=2),
                     in0=t,
                     in1=same[:].unsqueeze(1).to_broadcast([P, heads, PAIRS, 2]),
                 )
                 nc.vector.tensor_mul(
-                    out=crossed[:, first : first + width].rearrange(as_pairs, h=heads, e=2),
+                    out=crossed[:, lo - first : hi - first].rearrange(as_pairs, h=heads, e=2),
                     in0=t[:, :, :, ::-1],
                     in1=cross[:].unsqueeze(1).to_broadcast([P, heads, PAIRS, 2]),
                 )
-            if b == PE_SUM_BANK:
-                total = psum.tile([P, BANK], F32, name="total", tag="spare")
-                nc.tensor.matmul(out=total[:], lhsT=ident[:], rhs=straight[:], start=True, stop=False)
-                nc.tensor.matmul(out=total[:], lhsT=ident[:], rhs=crossed[:], start=False, stop=True)
-                summed = keep.tile([P, BANK], F32, name="summed")
-                nc.scalar.copy(out=summed[:], in_=total[:])
-                store(b, summed)
-                continue
-            if b < ROTARY_BANKS - 1:
-                nc.gpsimd.tensor_add(out=straight[:], in0=straight[:], in1=crossed[:])
-                store(b, straight)
-            else:
-                half_heads = HEADS_PER_BANK // 2
-                for part in range(2):
-                    cols = slice(part * BANK // 2, (part + 1) * BANK // 2)
-                    nc.vector.tensor_add(out=straight[:, cols], in0=straight[:, cols], in1=crossed[:, cols])
-                    nc.sync.dma_start(
-                        out=homes[b][part * half_heads : (part + 1) * half_heads].rearrange("h s f -> s h f"),
-                        in_=straight[:, cols].rearrange("s (h f) -> s h f", h=half_heads),
-                    )
+            return straight, crossed
+
+        for b in range(ROTARY_BANKS):
+            widths = [BANK] if b < ROTARY_BANKS - 1 else [BANK // 2, BANK // 2]
+            made = [(i * widths[0],) + products(b, i * widths[0], widths[i]) for i in range(len(widths))]
+            for first, straight, crossed in made:
+                if b == PE_SUM_BANK:
+                    total = psum.tile([P, BANK], F32, name="total", tag="spare")
+                    nc.tensor.matmul(out=total[:], lhsT=ident[:], rhs=straight[:], start=True, stop=False)
+                    nc.tensor.matmul(out=total[:], lhsT=ident[:], rhs=crossed[:], start=False, stop=True)
+                    summed = keep.tile([P, BANK], F32, name="summed")
+                    nc.scalar.copy(out=summed[:], in_=total[:])
+                    store(b, first, summed)
+                    continue
+                adder = nc.gpsimd if b < ROTARY_BANKS - 1 else nc.vector
+                adder.tensor_add(out=straight[:], in0=straight[:], in1=crossed[:])
+                store(b, first, straight)

@@ -22,7 +22,7 @@ ROTARY_BANKS = Q_BANKS + 1
 BANKS = ROTARY_BANKS + 1
 N_ALL = BANKS * BANK
 WORD_BYTES = 2
-PE_SUM_BANK = 1
+PE_SUM_BANKS = (1, 2)
 
 FLOPS = 2 * P * D * N_ALL
 
@@ -116,12 +116,12 @@ def tile_rlaattention_pa_s_kernel(
             heads = result.shape[1] // HD
             nc.sync.dma_start(
                 out=homes[b][first // HD : first // HD + heads].rearrange("h s f -> s h f"),
-                in_=result[:].rearrange("s (h f) -> s h f", h=heads),
+                in_=result.rearrange("s (h f) -> s h f", h=heads),
             )
 
         values = keep.tile([P, BANK], F32)
         nc.scalar.copy(out=values[:], in_=banks[ROTARY_BANKS][0][2][:])
-        store(ROTARY_BANKS, 0, values)
+        store(ROTARY_BANKS, 0, values[:])
 
         as_pairs = "s (h j e) -> s h j e"
 
@@ -147,18 +147,26 @@ def tile_rlaattention_pa_s_kernel(
                 )
             return straight, crossed
 
+        HALF = BANK // 2
         for b in range(ROTARY_BANKS):
-            widths = [BANK] if b < ROTARY_BANKS - 1 else [BANK // 2, BANK // 2]
-            made = [(i * widths[0],) + products(b, i * widths[0], widths[i]) for i in range(len(widths))]
-            for first, straight, crossed in made:
-                if b == PE_SUM_BANK:
-                    total = psum.tile([P, BANK], F32, name="total", tag="spare")
-                    nc.tensor.matmul(out=total[:], lhsT=ident[:], rhs=straight[:], start=True, stop=False)
-                    nc.tensor.matmul(out=total[:], lhsT=ident[:], rhs=crossed[:], start=False, stop=True)
-                    summed = keep.tile([P, BANK], F32, name="summed")
+            halves = []
+            if b in PE_SUM_BANKS:
+                straight, crossed = products(b, 0, BANK)
+                for first in (0, HALF):
+                    halves.append((first, straight[:, first : first + HALF], crossed[:, first : first + HALF]))
+            else:
+                for first in (0, HALF):
+                    straight, crossed = products(b, first, HALF)
+                    halves.append((first, straight[:], crossed[:]))
+            for first, straight, crossed in halves:
+                if b in PE_SUM_BANKS and first == HALF:
+                    total = psum.tile([P, HALF], F32, name="total%d" % b, tag="spare" if b == PE_SUM_BANKS[0] else "acc0_%d" % HD)
+                    nc.tensor.matmul(out=total[:], lhsT=ident[:], rhs=straight, start=True, stop=False)
+                    nc.tensor.matmul(out=total[:], lhsT=ident[:], rhs=crossed, start=False, stop=True)
+                    summed = keep.tile([P, HALF], F32, name="summed%d" % b)
                     nc.scalar.copy(out=summed[:], in_=total[:])
-                    store(b, first, summed)
+                    store(b, first, summed[:])
                     continue
                 adder = nc.gpsimd if b < ROTARY_BANKS - 1 else nc.vector
-                adder.tensor_add(out=straight[:], in0=straight[:], in1=crossed[:])
+                adder.tensor_add(out=straight, in0=straight, in1=crossed)
                 store(b, first, straight)

@@ -112,16 +112,16 @@ def tile_rlaattention_pa_s_kernel(
         homes.append(out_1[0])
         homes.append(out_2[0])
 
-        def store(b, first, result):
+        def store(b, first, result, queue):
             heads = result.shape[1] // HD
-            nc.sync.dma_start(
+            queue.dma_start(
                 out=homes[b][first // HD : first // HD + heads].rearrange("h s f -> s h f"),
                 in_=result.rearrange("s (h f) -> s h f", h=heads),
             )
 
         values = keep.tile([P, BANK], F32)
         nc.scalar.copy(out=values[:], in_=banks[ROTARY_BANKS][0][2][:])
-        store(ROTARY_BANKS, 0, values[:])
+        store(ROTARY_BANKS, 0, values[:], nc.scalar)
 
         as_pairs = "s (h j e) -> s h j e"
 
@@ -165,8 +165,9 @@ def tile_rlaattention_pa_s_kernel(
                     nc.tensor.matmul(out=total[:], lhsT=ident[:], rhs=crossed, start=False, stop=True)
                     summed = keep.tile([P, HALF], F32, name="summed%d" % b)
                     nc.scalar.copy(out=summed[:], in_=total[:])
-                    store(b, first, summed[:])
+                    store(b, first, summed[:], nc.scalar)
                     continue
                 adder = nc.gpsimd if b < ROTARY_BANKS - 1 else nc.vector
                 adder.tensor_add(out=straight, in0=straight, in1=crossed)
-                store(b, first, straight)
+                late = b >= ROTARY_BANKS - 2 and first == HALF
+                store(b, first, straight, nc.scalar if late else nc.sync)

@@ -62,7 +62,8 @@ def tile_rlaattention_pa_s_kernel(
                 in_=Wqkv_scales[0, 4 * quadrant : 4 * quadrant + 4, :].bitcast(I32),
             )
         load_words(1, 3)
-        load_words(3, BANKS)
+        load_words(ROTARY_BANKS, BANKS)
+        load_words(3, ROTARY_BANKS)
 
         ident = keep.tile([P, P], F32)
         make_identity(nc, ident[:])
@@ -86,8 +87,8 @@ def tile_rlaattention_pa_s_kernel(
         cross = keep.tile([P, PAIRS, 2], F32)
         nc.vector.tensor_mul(out=cross[:], in0=f_pairs[:, :, 0:1].to_broadcast([P, PAIRS, 2]), in1=signs[:])
 
-        banks = []
-        for b in range(BANKS):
+        banks = {}
+        for b in [0, 1, ROTARY_BANKS] + list(range(2, ROTARY_BANKS)):
             widths = [HD, HD, BANK // 2] if b == 0 else [BANK]
             pieces = []
             for width in widths:
@@ -106,7 +107,7 @@ def tile_rlaattention_pa_s_kernel(
                     stop=True,
                 )
                 pieces.append((first, width, acc))
-            banks.append(pieces)
+            banks[b] = pieces
 
         homes = [out_0[0, HEADS_PER_BANK * b : HEADS_PER_BANK * (b + 1)] for b in range(Q_BANKS)]
         homes.append(out_1[0])

@@ -168,7 +168,12 @@ def tile_rlaattention_pa_s_kernel(
                     nc.scalar.copy(out=summed[:], in_=total[:])
                     store(b, first, summed[:], nc.scalar)
                     continue
-                adder = nc.gpsimd if b < ROTARY_BANKS - 1 else nc.vector
-                adder.tensor_add(out=straight, in0=straight, in1=crossed)
-                late = b >= ROTARY_BANKS - 2 and first == HALF
-                store(b, first, straight, nc.scalar if late else nc.sync)
+                if b < ROTARY_BANKS - 1:
+                    nc.gpsimd.tensor_add(out=straight, in0=straight, in1=crossed)
+                    late = b == ROTARY_BANKS - 2 and first == HALF
+                    store(b, first, straight, nc.scalar if late else nc.sync)
+                    continue
+                for head in range(HALF // HD):
+                    cols = slice(head * HD, (head + 1) * HD)
+                    nc.vector.tensor_add(out=straight[:, cols], in0=straight[:, cols], in1=crossed[:, cols])
+                    store(b, first + head * HD, straight[:, cols], nc.scalar if head == 1 else nc.sync)

@@ -16,13 +16,15 @@ D = 512
 HD = 128
 PAIRS = HD // 2
 BANK = 512
+HALF = BANK // 2
 HEADS_PER_BANK = BANK // HD
 Q_BANKS = 4
 ROTARY_BANKS = Q_BANKS + 1
+LAST = ROTARY_BANKS - 1
 BANKS = ROTARY_BANKS + 1
 N_ALL = BANKS * BANK
 WORD_BYTES = 2
-PE_SUM_BANKS = (1, 2)
+TURNED = {(1, HALF): "spare", (2, HALF): "acc0_128", (3, HALF): "acc0_256"}
 
 FLOPS = 2 * P * D * N_ALL
 
@@ -67,6 +69,11 @@ def tile_rlaattention_pa_s_kernel(
 
         ident = keep.tile([P, P], F32)
         make_identity(nc, ident[:])
+        swap = keep.tile([P, P], F32)
+        nc.gpsimd.tensor_copy(
+            out=swap[:].rearrange("k (j e) -> k j e", e=2),
+            in_=ident[:].rearrange("k (j e) -> k j e", e=2)[:, :, ::-1],
+        )
         x_words = x_sb[:].bitcast(F32)
         xt = psum.tile([P, 2, P], F32, tag="spare")
         for u in range(2):
@@ -86,28 +93,50 @@ def tile_rlaattention_pa_s_kernel(
         nc.vector.tensor_copy(out=same[:], in_=f_pairs[:, :, 1:2].to_broadcast([P, PAIRS, 2]))
         cross = keep.tile([P, PAIRS, 2], F32)
         nc.vector.tensor_mul(out=cross[:], in0=f_pairs[:, :, 0:1].to_broadcast([P, PAIRS, 2]), in1=signs[:])
+        tables_t = psum.tile([P, 2, P], F32, tag="acc4_0")
+        nc.tensor.transpose(tables_t[:, 0, :], same[:].rearrange("s j e -> s (j e)"), ident[:])
+        nc.tensor.transpose(tables_t[:, 1, :], cross[:].rearrange("s j e -> s (j e)"), ident[:])
+        same_t = keep.tile([P, P], F32)
+        nc.scalar.copy(out=same_t[:], in_=tables_t[:, 0, :])
+        cross_t = keep.tile([P, P], F32)
+        nc.scalar.mul(out=cross_t[:], in_=tables_t[:, 1, :], mul=-1.0)
+
+        def multiply(out, first_col, width, w_stationary):
+            cols = slice(first_col, first_col + width)
+            w = dict(
+                data=w_words[:, WORD_BYTES * cols.start : WORD_BYTES * cols.stop].bitcast(FP4X4),
+                scale=w_scales[:, cols],
+            )
+            xq = dict(data=x_codes[:].bitcast(FP8X4), scale=x_scales[:])
+            stationary, moving = (w, xq) if w_stationary else (xq, w)
+            nc.tensor.matmul_mx(
+                out=out,
+                lhsT=stationary["data"],
+                lhsT_scale=stationary["scale"],
+                rhs=moving["data"],
+                rhs_scale=moving["scale"],
+                start=True,
+                stop=True,
+            )
 
         banks = {}
-        for b in [0, 1, ROTARY_BANKS] + list(range(2, ROTARY_BANKS)):
-            widths = [HD, HD, BANK // 2] if b == 0 else [BANK]
-            pieces = []
-            for width in widths:
-                first = sum(piece[1] for piece in pieces)
-                cols = slice(BANK * b + first, BANK * b + first + width)
-                acc = psum.tile(
-                    [P, width], F32, name="acc%d_%d" % (b, first), tag="spare" if cols.start == 0 else "acc%d_%d" % (b, first)
-                )
-                nc.tensor.matmul_mx(
-                    out=acc[:],
-                    lhsT=x_codes[:].bitcast(FP8X4),
-                    lhsT_scale=x_scales[:],
-                    rhs=w_words[:, WORD_BYTES * cols.start : WORD_BYTES * cols.stop].bitcast(FP4X4),
-                    rhs_scale=w_scales[:, cols],
-                    start=True,
-                    stop=True,
-                )
-                pieces.append((first, width, acc))
-            banks[b] = pieces
+        banks[0] = []
+        for first, width in ((0, HD), (HD, HD), (HALF, HALF)):
+            acc = psum.tile([P, width], F32, name="acc0_%d" % first, tag="spare" if first == 0 else "acc0_%d" % first)
+            multiply(acc[:], first, width, False)
+            banks[0].append((first, width, acc))
+        for b in [1, ROTARY_BANKS] + list(range(2, ROTARY_BANKS)):
+            acc = psum.tile([P, BANK], F32, name="acc%d_0" % b, tag="acc%d_0" % b)
+            banks[b] = [(0, BANK, acc)]
+            if b == ROTARY_BANKS:
+                multiply(acc[:], BANK * b, BANK, False)
+                continue
+            for first in (0, HALF):
+                if (b, first) in TURNED:
+                    for head_first in (first, first + HD):
+                        multiply(acc[:, head_first : head_first + HD], BANK * b + head_first, HD, True)
+                else:
+                    multiply(acc[:, first : first + HALF], BANK * b + first, HALF, False)
 
         homes = [out_0[0, HEADS_PER_BANK * b : HEADS_PER_BANK * (b + 1)] for b in range(Q_BANKS)]
         homes.append(out_1[0])
@@ -126,12 +155,23 @@ def tile_rlaattention_pa_s_kernel(
 
         as_pairs = "s (h j e) -> s h j e"
 
-        def products(b, first, width):
-            straight = keep.tile([P, width], F32, name="straight%d_%d" % (b, first))
-            crossed = keep.tile([P, width], F32, name="crossed%d_%d" % (b, first))
+        def products(b, first):
+            straight = keep.tile([P, HALF], F32, name="straight%d_%d" % (b, first))
+            crossed = keep.tile([P, HALF], F32, name="crossed%d_%d" % (b, first))
+            if (b, first) in TURNED:
+                by_head = [P, HALF // HD, P]
+                as_heads = "f (h s) -> f h s"
+                t = banks[b][0][2][:, first : first + HALF].rearrange(as_heads, s=P)
+                nc.vector.tensor_mul(
+                    out=straight[:].rearrange(as_heads, s=P), in0=t, in1=same_t[:].unsqueeze(1).to_broadcast(by_head)
+                )
+                nc.vector.tensor_mul(
+                    out=crossed[:].rearrange(as_heads, s=P), in0=t, in1=cross_t[:].unsqueeze(1).to_broadcast(by_head)
+                )
+                return straight, crossed
             for piece_first, piece_width, acc in banks[b]:
                 lo = max(first, piece_first)
-                hi = min(first + width, piece_first + piece_width)
+                hi = min(first + HALF, piece_first + piece_width)
                 if lo >= hi:
                     continue
                 heads = (hi - lo) // HD
@@ -148,32 +188,27 @@ def tile_rlaattention_pa_s_kernel(
                 )
             return straight, crossed
 
-        HALF = BANK // 2
         for b in range(ROTARY_BANKS):
-            halves = []
-            if b in PE_SUM_BANKS:
-                straight, crossed = products(b, 0, BANK)
-                for first in (0, HALF):
-                    halves.append((first, straight[:, first : first + HALF], crossed[:, first : first + HALF]))
-            else:
-                for first in (0, HALF):
-                    straight, crossed = products(b, first, HALF)
-                    halves.append((first, straight[:], crossed[:]))
-            for first, straight, crossed in halves:
-                if b in PE_SUM_BANKS and first == HALF:
-                    total = psum.tile([P, HALF], F32, name="total%d" % b, tag="spare" if b == PE_SUM_BANKS[0] else "acc0_%d" % HD)
-                    nc.tensor.matmul(out=total[:], lhsT=ident[:], rhs=straight, start=True, stop=False)
-                    nc.tensor.matmul(out=total[:], lhsT=ident[:], rhs=crossed, start=False, stop=True)
+            made = [(first,) + products(b, first) for first in (0, HALF)]
+            for first, straight, crossed in made:
+                if (b, first) in TURNED:
+                    total = psum.tile([P, HALF], F32, name="total%d" % b, tag=TURNED[(b, first)])
+                    for head in range(HALF // HD):
+                        cols = slice(head * HD, (head + 1) * HD)
+                        nc.tensor.matmul(
+                            out=total[:, cols], lhsT=straight[:, cols], rhs=ident[:], is_transpose=True, start=True, stop=False
+                        )
+                        nc.tensor.matmul(
+                            out=total[:, cols], lhsT=crossed[:, cols], rhs=swap[:], is_transpose=True, start=False, stop=True
+                        )
                     summed = keep.tile([P, HALF], F32, name="summed%d" % b)
                     nc.scalar.copy(out=summed[:], in_=total[:])
                     store(b, first, summed[:], nc.scalar)
-                    continue
-                if b < ROTARY_BANKS - 1:
-                    nc.gpsimd.tensor_add(out=straight, in0=straight, in1=crossed)
-                    late = b == ROTARY_BANKS - 2 and first == HALF
-                    store(b, first, straight, nc.scalar if late else nc.sync)
-                    continue
-                for head in range(HALF // HD):
-                    cols = slice(head * HD, (head + 1) * HD)
-                    nc.vector.tensor_add(out=straight[:, cols], in0=straight[:, cols], in1=crossed[:, cols])
-                    store(b, first + head * HD, straight[:, cols], nc.scalar if head == 1 else nc.sync)
+                elif b < LAST:
+                    nc.gpsimd.tensor_add(out=straight[:], in0=straight[:], in1=crossed[:])
+                    store(b, first, straight[:], nc.sync)
+                else:
+                    for head, queue in enumerate((nc.sync, nc.scalar)):
+                        cols = slice(head * HD, (head + 1) * HD)
+                        nc.vector.tensor_add(out=straight[:, cols], in0=straight[:, cols], in1=crossed[:, cols])
+                        store(b, first + head * HD, straight[:, cols], queue)

@@ -96,10 +96,10 @@ def tile_rlaattention_pa_s_kernel(
         tables_t = psum.tile([P, 2, P], F32, tag="acc4_0")
         nc.tensor.transpose(tables_t[:, 0, :], same[:].rearrange("s j e -> s (j e)"), ident[:])
         nc.tensor.transpose(tables_t[:, 1, :], cross[:].rearrange("s j e -> s (j e)"), ident[:])
-        same_t = keep.tile([P, P], F32)
-        nc.scalar.copy(out=same_t[:], in_=tables_t[:, 0, :])
-        cross_t = keep.tile([P, P], F32)
-        nc.scalar.mul(out=cross_t[:], in_=tables_t[:, 1, :], mul=-1.0)
+        same_t = keep.tile([P, 2, P // 2], F32)
+        nc.scalar.copy(out=same_t[:], in_=tables_t[:, 0, :].rearrange("f (q e) -> f e q", e=2))
+        cross_t = keep.tile([P, 2, P // 2], F32)
+        nc.scalar.mul(out=cross_t[:], in_=tables_t[:, 1, :].rearrange("f (q e) -> f e q", e=2), mul=-1.0)
 
         def multiply(out, first_col, width, w_stationary):
             cols = slice(first_col, first_col + width)
@@ -159,14 +159,17 @@ def tile_rlaattention_pa_s_kernel(
             straight = keep.tile([P, HALF], F32, name="straight%d_%d" % (b, first))
             crossed = keep.tile([P, HALF], F32, name="crossed%d_%d" % (b, first))
             if (b, first) in TURNED:
-                by_head = [P, HALF // HD, P]
-                as_heads = "f (h s) -> f h s"
-                t = banks[b][0][2][:, first : first + HALF].rearrange(as_heads, s=P)
+                shape = [P, 2, HALF // HD, P // 2]
+                t = banks[b][0][2][:, first : first + HALF].rearrange("f (h q e) -> f e h q", h=HALF // HD, e=2)
                 nc.vector.tensor_mul(
-                    out=straight[:].rearrange(as_heads, s=P), in0=t, in1=same_t[:].unsqueeze(1).to_broadcast(by_head)
+                    out=straight[:].rearrange("f (e h q) -> f e h q", e=2, h=HALF // HD),
+                    in0=t,
+                    in1=same_t[:].unsqueeze(2).to_broadcast(shape),
                 )
                 nc.vector.tensor_mul(
-                    out=crossed[:].rearrange(as_heads, s=P), in0=t, in1=cross_t[:].unsqueeze(1).to_broadcast(by_head)
+                    out=crossed[:].rearrange("f (e h q) -> f e h q", e=2, h=HALF // HD),
+                    in0=t,
+                    in1=cross_t[:].unsqueeze(2).to_broadcast(shape),
                 )
                 return straight, crossed
             for piece_first, piece_width, acc in banks[b]:
@@ -203,7 +206,10 @@ def tile_rlaattention_pa_s_kernel(
                         )
                     summed = keep.tile([P, HALF], F32, name="summed%d" % b)
                     nc.scalar.copy(out=summed[:], in_=total[:])
-                    store(b, first, summed[:], nc.scalar)
+                    nc.scalar.dma_start(
+                        out=homes[b][first // HD : first // HD + HALF // HD].rearrange("h (q e) f -> (h q) (e f)", e=2),
+                        in_=summed[:],
+                    )
                 elif b < LAST:
                     nc.gpsimd.tensor_add(out=straight[:], in0=straight[:], in1=crossed[:])
                     store(b, first, straight[:], nc.sync)

from contextlib import ExitStack

import concourse.mybir as mybir
from concourse.masks import make_identity

F32 = mybir.dt.float32
BF16 = mybir.dt.bfloat16
I32 = mybir.dt.int32
U32 = mybir.dt.uint32
U8 = mybir.dt.uint8
FP8X4 = mybir.dt.float8_e4m3fn_x4
FP4X4 = mybir.dt.float4_e2m1fn_x4

P = 128
D = 512
HD = 128
PAIRS = HD // 2
BANK = 512
HALF = BANK // 2
HEADS_PER_BANK = BANK // HD
Q_BANKS = 4
ROTARY_BANKS = Q_BANKS + 1
LAST = ROTARY_BANKS - 1
BANKS = ROTARY_BANKS + 1
N_ALL = BANKS * BANK
WORD_BYTES = 2
TURNED = {(1, HALF): "spare", (2, HALF): "acc0_128", (3, HALF): "acc0_256"}

FLOPS = 2 * P * D * N_ALL


def tile_rlaattention_pa_s_kernel(
    tc, x, freqs_cis, Wqkv_words, Wqkv_scales, out_0, out_1, out_2
):
    nc = tc.nc
    with ExitStack() as ctx:
        keep = ctx.enter_context(tc.tile_pool(name="keep", bufs=1))
        psum = ctx.enter_context(tc.psum_pool(name="psum", bufs=1))

        w_scales = keep.tile([P, N_ALL], U8, align_bytes=64)
        nc.vector.memset(w_scales[:].bitcast(I32), 0)

        signs = keep.tile([P, PAIRS, 2], F32)
        nc.vector.memset(signs[:, :, 0:1], -1.0)
        nc.vector.memset(signs[:, :, 1:2], 1.0)

        x_sb = keep.tile([P, D], BF16)
        nc.sync.dma_start(out=x_sb[:], in_=x[0])
        f_sb = keep.tile([P, HD], BF16)
        nc.scalar.dma_start(out=f_sb[:], in_=freqs_cis)

        w_words = keep.tile([P, WORD_BYTES * N_ALL], U8, align_bytes=64)

        def load_words(first_bank, end_bank):
            cols = slice(WORD_BYTES * BANK * first_bank, WORD_BYTES * BANK * end_bank)
            nc.sync.dma_start(
                out=w_words[:, cols].bitcast(I32), in_=Wqkv_words[0][:, cols].bitcast(I32)
            )

        load_words(0, 1)
        for quadrant in range(4):
            nc.sync.dma_start(
                out=w_scales[32 * quadrant : 32 * quadrant + 4, :].bitcast(I32),
                in_=Wqkv_scales[0, 4 * quadrant : 4 * quadrant + 4, :].bitcast(I32),
            )
        load_words(1, 3)
        load_words(ROTARY_BANKS, BANKS)
        load_words(3, ROTARY_BANKS)

        ident = keep.tile([P, P], F32)
        make_identity(nc, ident[:])
        swap = keep.tile([P, P], F32)
        nc.gpsimd.tensor_copy(
            out=swap[:].rearrange("k (j e) -> k j e", e=2),
            in_=ident[:].rearrange("k (j e) -> k j e", e=2)[:, :, ::-1],
        )
        x_words = x_sb[:].bitcast(F32)
        xt = psum.tile([P, 2, P], F32, tag="spare")
        for u in range(2):
            nc.tensor.transpose(xt[:, u, :], x_words[:, u : D // 2 : 2], ident[:])
        x_grouped = keep.tile([P, P, 2], F32, align_bytes=64)
        nc.scalar.copy(out=x_grouped[:], in_=xt[:].rearrange("p u s -> p s u"))
        x_codes = keep.tile([P, P], U32, align_bytes=64)
        x_scales = keep.tile([P, P], U8, align_bytes=64)
        nc.vector.quantize_mx(
            out=x_codes[:].bitcast(FP8X4),
            scales=x_scales[:],
            in_=x_grouped[:].rearrange("p s u -> p (s u)").bitcast(BF16),
        )

        f_pairs = f_sb[:].rearrange("s (j e) -> s j e", e=2)
        same = keep.tile([P, PAIRS, 2], F32)
        nc.vector.tensor_copy(out=same[:], in_=f_pairs[:, :, 1:2].to_broadcast([P, PAIRS, 2]))
        cross = keep.tile([P, PAIRS, 2], F32)
        nc.vector.tensor_mul(out=cross[:], in0=f_pairs[:, :, 0:1].to_broadcast([P, PAIRS, 2]), in1=signs[:])
        tables_t = psum.tile([P, 2, P], F32, tag="acc4_0")
        nc.tensor.transpose(tables_t[:, 0, :], same[:].rearrange("s j e -> s (j e)"), ident[:])
        nc.tensor.transpose(tables_t[:, 1, :], cross[:].rearrange("s j e -> s (j e)"), ident[:])
        same_t = keep.tile([P, 2, P // 2], F32)
        nc.scalar.copy(out=same_t[:], in_=tables_t[:, 0, :].rearrange("f (q e) -> f e q", e=2))
        cross_t = keep.tile([P, 2, P // 2], F32)
        nc.scalar.mul(out=cross_t[:], in_=tables_t[:, 1, :].rearrange("f (q e) -> f e q", e=2), mul=-1.0)

        def multiply(out, first_col, width, w_stationary):
            cols = slice(first_col, first_col + width)
            w = dict(
                data=w_words[:, WORD_BYTES * cols.start : WORD_BYTES * cols.stop].bitcast(FP4X4),
                scale=w_scales[:, cols],
            )
            xq = dict(data=x_codes[:].bitcast(FP8X4), scale=x_scales[:])
            stationary, moving = (w, xq) if w_stationary else (xq, w)
            nc.tensor.matmul_mx(
                out=out,
                lhsT=stationary["data"],
                lhsT_scale=stationary["scale"],
                rhs=moving["data"],
                rhs_scale=moving["scale"],
                start=True,
                stop=True,
            )

        banks = {}
        banks[0] = []
        for first, width in ((0, HD), (HD, HD), (HALF, HALF)):
            acc = psum.tile([P, width], F32, name="acc0_%d" % first, tag="spare" if first == 0 else "acc0_%d" % first)
            multiply(acc[:], first, width, False)
            banks[0].append((first, width, acc))
        for b in [1, ROTARY_BANKS] + list(range(2, ROTARY_BANKS)):
            acc = psum.tile([P, BANK], F32, name="acc%d_0" % b, tag="acc%d_0" % b)
            banks[b] = [(0, BANK, acc)]
            if b == ROTARY_BANKS:
                multiply(acc[:], BANK * b, BANK, False)
                continue
            for first in (0, HALF):
                if (b, first) in TURNED:
                    for head_first in (first, first + HD):
                        multiply(acc[:, head_first : head_first + HD], BANK * b + head_first, HD, True)
                else:
                    multiply(acc[:, first : first + HALF], BANK * b + first, HALF, False)

        homes = [out_0[0, HEADS_PER_BANK * b : HEADS_PER_BANK * (b + 1)] for b in range(Q_BANKS)]
        homes.append(out_1[0])
        homes.append(out_2[0])

        def store(b, first, result, queue):
            heads = result.shape[1] // HD
            queue.dma_start(
                out=homes[b][first // HD : first // HD + heads].rearrange("h s f -> s h f"),
                in_=result.rearrange("s (h f) -> s h f", h=heads),
            )

        values = keep.tile([P, BANK], F32)
        nc.scalar.copy(out=values[:], in_=banks[ROTARY_BANKS][0][2][:])
        store(ROTARY_BANKS, 0, values[:], nc.scalar)

        as_pairs = "s (h j e) -> s h j e"

        def products(b, first):
            straight = keep.tile([P, HALF], F32, name="straight%d_%d" % (b, first))
            crossed = keep.tile([P, HALF], F32, name="crossed%d_%d" % (b, first))
            if (b, first) in TURNED:
                shape = [P, 2, HALF // HD, P // 2]
                t = banks[b][0][2][:, first : first + HALF].rearrange("f (h q e) -> f e h q", h=HALF // HD, e=2)
                nc.vector.tensor_mul(
                    out=straight[:].rearrange("f (e h q) -> f e h q", e=2, h=HALF // HD),
                    in0=t,
                    in1=same_t[:].unsqueeze(2).to_broadcast(shape),
                )
                nc.vector.tensor_mul(
                    out=crossed[:].rearrange("f (e h q) -> f e h q", e=2, h=HALF // HD),
                    in0=t,
                    in1=cross_t[:].unsqueeze(2).to_broadcast(shape),
                )
                return straight, crossed
            for piece_first, piece_width, acc in banks[b]:
                lo = max(first, piece_first)
                hi = min(first + HALF, piece_first + piece_width)
                if lo >= hi:
                    continue
                heads = (hi - lo) // HD
                t = acc[:, lo - piece_first : hi - piece_first].rearrange(as_pairs, h=heads, e=2)
                nc.vector.tensor_mul(
                    out=straight[:, lo - first : hi - first].rearrange(as_pairs, h=heads, e=2),
                    in0=t,
                    in1=same[:].unsqueeze(1).to_broadcast([P, heads, PAIRS, 2]),
                )
                nc.vector.tensor_mul(
                    out=crossed[:, lo - first : hi - first].rearrange(as_pairs, h=heads, e=2),
                    in0=t[:, :, :, ::-1],
                    in1=cross[:].unsqueeze(1).to_broadcast([P, heads, PAIRS, 2]),
                )
            return straight, crossed

        for b in range(ROTARY_BANKS):
            made = [(first,) + products(b, first) for first in (0, HALF)]
            for first, straight, crossed in made:
                if (b, first) in TURNED:
                    total = psum.tile([P, HALF], F32, name="total%d" % b, tag=TURNED[(b, first)])
                    for head in range(HALF // HD):
                        cols = slice(head * HD, (head + 1) * HD)
                        nc.tensor.matmul(
                            out=total[:, cols], lhsT=straight[:, cols], rhs=ident[:], is_transpose=True, start=True, stop=False
                        )
                        nc.tensor.matmul(
                            out=total[:, cols], lhsT=crossed[:, cols], rhs=swap[:], is_transpose=True, start=False, stop=True
                        )
                    summed = keep.tile([P, HALF], F32, name="summed%d" % b)
                    nc.scalar.copy(out=summed[:], in_=total[:])
                    nc.scalar.dma_start(
                        out=homes[b][first // HD : first // HD + HALF // HD].rearrange("h (q e) f -> (h q) (e f)", e=2),
                        in_=summed[:],
                    )
                elif b < LAST:
                    nc.gpsimd.tensor_add(out=straight[:], in0=straight[:], in1=crossed[:])
                    store(b, first, straight[:], nc.sync)
                else:
                    for head, queue in enumerate((nc.sync, nc.scalar)):
                        cols = slice(head * HD, (head + 1) * HD)
                        nc.vector.tensor_add(out=straight[:, cols], in0=straight[:, cols], in1=crossed[:, cols])
                        store(b, first + head * HD, straight[:, cols], queue)
